import numpy as np
import ml_dtypes

BF16 = ml_dtypes.bfloat16


def bf(x):
    return np.asarray(x, np.float32).astype(BF16)


def f32(x):
    return np.asarray(x, np.float32)


def f64(x):
    return np.asarray(x).astype(np.float64)


def striped(idx):
    return np.tile(idx.reshape(-1, 16).T, (8, 1))


B, W, D, H, C, S, N = 8, 128, 16, 64, 1024, 1024, 64


def setup_inputs():
    x = f32(0.5 * np.random.standard_normal((C, S)))
    query = f32(0.125 * x + 0.5 * np.random.standard_normal((C, S)))
    return {"x": x, "query": query, "offs": striped(np.random.permutation(S)[:N])}


def reference(x, query, offs):
    idx = offs[:16].T.reshape(-1)
    t = f64(x).reshape(B, W, S)
    picked = t[:, :, idx]
    other = t[::-1, :, :N]
    sim = (picked * other).sum(axis=1)
    dist_mean = 1.0 - (f64(query) * f64(x)).sum() / (B * W * H)
    return np.reshape(dist_mean + np.maximum(sim, 0.0).mean(), (1, 1))

@@ -1,0 +1,87 @@
+import concourse.mybir as mybir
+
+F32 = mybir.dt.float32
+U16 = mybir.dt.uint16
+MULT = mybir.AluOpType.mult
+ADD = mybir.AluOpType.add
+RELU = mybir.ActivationFunctionType.Relu
+
+P = 128
+IMAGES = 8
+PAIRS = IMAGES // 2
+S = 1024
+N = 64
+PLACES = 65536
+SIMS = IMAGES * N
+
+FLOPS = 2 * IMAGES * P * S + 2 * IMAGES * P * N
+
+
+def tile_scaleinvariantreconstructionloss_kernel(tc, x, query, offs, out):
+    nc = tc.nc
+    with (
+        tc.tile_pool(name="held", bufs=1) as held,
+        tc.tile_pool(name="scratch", bufs=2) as scratch,
+        tc.psum_pool(name="psum", bufs=1) as psum,
+    ):
+        offsets = held.tile([P, N // 16], U16, name="offsets")
+        nc.sync.dma_start(offsets[:], offs)
+        x_tiles = [held.tile([P, S], F32, name=f"x{b}") for b in range(IMAGES)]
+        q_tiles = [held.tile([P, S], F32, name=f"q{b}") for b in range(IMAGES)]
+        for b in range(IMAGES):
+            nc.sync.dma_start(x_tiles[b][:], x[b * P : (b + 1) * P, :])
+            nc.sync.dma_start(q_tiles[b][:], query[b * P : (b + 1) * P, :])
+
+        ones = held.tile([P, 1], F32, name="ones")
+        nc.vector.memset(ones[:], 1.0)
+        dot_weight = held.tile([P, 1], F32, name="dot_weight")
+        nc.vector.memset(dot_weight[:], -1.0 / PLACES)
+        penalty_weight = held.tile([P, 1], F32, name="penalty_weight")
+        nc.vector.memset(penalty_weight[:], 1.0 / SIMS)
+
+        dot_sums = held.tile([P, IMAGES], F32, name="dot_sums")
+        sim = psum.tile([P, PAIRS], F32, name="sim")
+
+        for b in range(IMAGES):
+            mirror = IMAGES - 1 - b
+            if mirror < b:
+                picked_times_mirror = scratch.tile([P, 2 * N], F32, name="picked_times_mirror")
+                nc.vector.tensor_tensor(
+                    picked_times_mirror[:, 0:N],
+                    x_tiles[mirror][:].indirect(offsets[:]),
+                    x_tiles[b][:, 0:N],
+                    MULT,
+                )
+                nc.vector.tensor_tensor(
+                    picked_times_mirror[:, N : 2 * N],
+                    x_tiles[b][:].indirect(offsets[:]),
+                    x_tiles[mirror][:, 0:N],
+                    MULT,
+                )
+                nc.tensor.matmul(
+                    sim[:, mirror : mirror + 1], picked_times_mirror[:], ones[:], start=True, stop=True
+                )
+
+            q_times_x = scratch.tile([P, S], F32, name="q_times_x")
+            nc.vector.scalar_tensor_tensor(
+                q_times_x[:],
+                q_tiles[b][:],
+                1.0,
+                x_tiles[b][:],
+                MULT,
+                MULT,
+                accum_out=dot_sums[:, b : b + 1],
+            )
+
+        positive_sim = held.tile([P, PAIRS], F32, name="positive_sim")
+        penalty_sums = held.tile([P, 1], F32, name="penalty_sums")
+        nc.scalar.activation(positive_sim[:], sim[:], RELU, accum_out=penalty_sums[:])
+
+        terms = psum.tile([1, IMAGES + 1], F32, name="terms")
+        nc.tensor.matmul(terms[:, IMAGES : IMAGES + 1], penalty_weight[:], penalty_sums[:], start=True, stop=True)
+        nc.tensor.matmul(terms[:, 0:IMAGES], dot_weight[:], dot_sums[:], start=True, stop=True)
+
+        terms_copy = held.tile([1, IMAGES + 1], F32, name="terms_copy")
+        loss = held.tile([1, 1], F32, name="loss")
+        nc.vector.tensor_scalar(terms_copy[:], terms[:], 1.0, 1.0, MULT, ADD, accum_out=loss[:])
+        nc.sync.dma_start(out, loss[:])

@@ -30,7 +30,8 @@ def tile_scaleinvariantreconstructionloss_kernel(tc, x, query, offs, out):
         q_tiles = [held.tile([P, S], F32, name=f"q{b}") for b in range(IMAGES)]
         for b in range(IMAGES):
             nc.sync.dma_start(x_tiles[b][:], x[b * P : (b + 1) * P, :])
-            nc.sync.dma_start(q_tiles[b][:], query[b * P : (b + 1) * P, :])
+            query_queue = nc.scalar if b < IMAGES - 1 else nc.sync
+            query_queue.dma_start(q_tiles[b][:], query[b * P : (b + 1) * P, :])
 
         ones = held.tile([P, 1], F32, name="ones")
         nc.vector.memset(ones[:], 1.0)

@@ -13,6 +13,9 @@ S = 1024
 N = 64
 PLACES = 65536
 SIMS = IMAGES * N
+HALF = S // 2
+
+QUERY_PIECES = [(b, 0, S) for b in range(IMAGES - 1)] + [(IMAGES - 1, 0, HALF), (IMAGES - 1, HALF, HALF)]
 
 FLOPS = 2 * IMAGES * P * S + 2 * IMAGES * P * N
 
@@ -30,8 +33,11 @@ def tile_scaleinvariantreconstructionloss_kernel(tc, x, query, offs, out):
         q_tiles = [held.tile([P, S], F32, name=f"q{b}") for b in range(IMAGES)]
         for b in range(IMAGES):
             nc.sync.dma_start(x_tiles[b][:], x[b * P : (b + 1) * P, :])
+        for b, first, columns in QUERY_PIECES:
             query_queue = nc.scalar if b < IMAGES - 1 else nc.sync
-            query_queue.dma_start(q_tiles[b][:], query[b * P : (b + 1) * P, :])
+            query_queue.dma_start(
+                q_tiles[b][:, first : first + columns], query[b * P : (b + 1) * P, first : first + columns]
+            )
 
         ones = held.tile([P, 1], F32, name="ones")
         nc.vector.memset(ones[:], 1.0)
@@ -40,7 +46,7 @@ def tile_scaleinvariantreconstructionloss_kernel(tc, x, query, offs, out):
         penalty_weight = held.tile([P, 1], F32, name="penalty_weight")
         nc.vector.memset(penalty_weight[:], 1.0 / SIMS)
 
-        dot_sums = held.tile([P, IMAGES], F32, name="dot_sums")
+        dot_sums = held.tile([P, len(QUERY_PIECES)], F32, name="dot_sums")
         sim = psum.tile([P, PAIRS], F32, name="sim")
 
         for b in range(IMAGES):
@@ -63,26 +69,29 @@ def tile_scaleinvariantreconstructionloss_kernel(tc, x, query, offs, out):
                     sim[:, mirror : mirror + 1], picked_times_mirror[:], ones[:], start=True, stop=True
                 )
 
-            q_times_x = scratch.tile([P, S], F32, name="q_times_x")
-            nc.vector.scalar_tensor_tensor(
-                q_times_x[:],
-                q_tiles[b][:],
-                1.0,
-                x_tiles[b][:],
-                MULT,
-                MULT,
-                accum_out=dot_sums[:, b : b + 1],
-            )
+            for piece, (image, first, columns) in enumerate(QUERY_PIECES):
+                if image == b:
+                    q_times_x = scratch.tile([P, S], F32, name="q_times_x")
+                    nc.vector.scalar_tensor_tensor(
+                        q_times_x[:, 0:columns],
+                        q_tiles[b][:, first : first + columns],
+                        1.0,
+                        x_tiles[b][:, first : first + columns],
+                        MULT,
+                        MULT,
+                        accum_out=dot_sums[:, piece : piece + 1],
+                    )
 
         positive_sim = held.tile([P, PAIRS], F32, name="positive_sim")
         penalty_sums = held.tile([P, 1], F32, name="penalty_sums")
         nc.scalar.activation(positive_sim[:], sim[:], RELU, accum_out=penalty_sums[:])
 
-        terms = psum.tile([1, IMAGES + 1], F32, name="terms")
-        nc.tensor.matmul(terms[:, IMAGES : IMAGES + 1], penalty_weight[:], penalty_sums[:], start=True, stop=True)
-        nc.tensor.matmul(terms[:, 0:IMAGES], dot_weight[:], dot_sums[:], start=True, stop=True)
+        pieces = len(QUERY_PIECES)
+        terms = psum.tile([1, pieces + 1], F32, name="terms")
+        nc.tensor.matmul(terms[:, pieces : pieces + 1], penalty_weight[:], penalty_sums[:], start=True, stop=True)
+        nc.tensor.matmul(terms[:, 0:pieces], dot_weight[:], dot_sums[:], start=True, stop=True)
 
-        terms_copy = held.tile([1, IMAGES + 1], F32, name="terms_copy")
+        terms_copy = held.tile([1, pieces + 1], F32, name="terms_copy")
         loss = held.tile([1, 1], F32, name="loss")
         nc.vector.tensor_scalar(terms_copy[:], terms[:], 1.0, 1.0, MULT, ADD, accum_out=loss[:])
         nc.sync.dma_start(out, loss[:])

@@ -33,11 +33,12 @@ def tile_scaleinvariantreconstructionloss_kernel(tc, x, query, offs, out):
         q_tiles = [held.tile([P, S], F32, name=f"q{b}") for b in range(IMAGES)]
         for b in range(IMAGES):
             nc.sync.dma_start(x_tiles[b][:], x[b * P : (b + 1) * P, :])
-        for b, first, columns in QUERY_PIECES:
             query_queue = nc.scalar if b < IMAGES - 1 else nc.sync
-            query_queue.dma_start(
-                q_tiles[b][:, first : first + columns], query[b * P : (b + 1) * P, first : first + columns]
-            )
+            for image, first, columns in QUERY_PIECES:
+                if image == b:
+                    query_queue.dma_start(
+                        q_tiles[b][:, first : first + columns], query[b * P : (b + 1) * P, first : first + columns]
+                    )
 
         ones = held.tile([P, 1], F32, name="ones")
         nc.vector.memset(ones[:], 1.0)

@@ -13,9 +13,8 @@ S = 1024
 N = 64
 PLACES = 65536
 SIMS = IMAGES * N
-HALF = S // 2
 
-QUERY_PIECES = [(b, 0, S) for b in range(IMAGES - 1)] + [(IMAGES - 1, 0, HALF), (IMAGES - 1, HALF, HALF)]
+IMAGE_ORDER = [b for k in range(PAIRS) for b in (k, IMAGES - 1 - k)]
 
 FLOPS = 2 * IMAGES * P * S + 2 * IMAGES * P * N
 
@@ -27,18 +26,15 @@ def tile_scaleinvariantreconstructionloss_kernel(tc, x, query, offs, out):
         tc.tile_pool(name="scratch", bufs=2) as scratch,
         tc.psum_pool(name="psum", bufs=1) as psum,
     ):
+        last_image = IMAGE_ORDER[-1]
         offsets = held.tile([P, N // 16], U16, name="offsets")
         nc.sync.dma_start(offsets[:], offs)
         x_tiles = [held.tile([P, S], F32, name=f"x{b}") for b in range(IMAGES)]
         q_tiles = [held.tile([P, S], F32, name=f"q{b}") for b in range(IMAGES)]
-        for b in range(IMAGES):
+        for b in IMAGE_ORDER:
             nc.sync.dma_start(x_tiles[b][:], x[b * P : (b + 1) * P, :])
-            query_queue = nc.scalar if b < IMAGES - 1 else nc.sync
-            for image, first, columns in QUERY_PIECES:
-                if image == b:
-                    query_queue.dma_start(
-                        q_tiles[b][:, first : first + columns], query[b * P : (b + 1) * P, first : first + columns]
-                    )
+            query_queue = nc.sync if b == last_image else nc.scalar
+            query_queue.dma_start(q_tiles[b][:], query[b * P : (b + 1) * P, :])
 
         ones = held.tile([P, 1], F32, name="ones")
         nc.vector.memset(ones[:], 1.0)
@@ -47,10 +43,10 @@ def tile_scaleinvariantreconstructionloss_kernel(tc, x, query, offs, out):
         penalty_weight = held.tile([P, 1], F32, name="penalty_weight")
         nc.vector.memset(penalty_weight[:], 1.0 / SIMS)
 
-        dot_sums = held.tile([P, len(QUERY_PIECES)], F32, name="dot_sums")
+        dot_sums = held.tile([P, IMAGES], F32, name="dot_sums")
         sim = psum.tile([P, PAIRS], F32, name="sim")
 
-        for b in range(IMAGES):
+        for b in IMAGE_ORDER:
             mirror = IMAGES - 1 - b
             if mirror < b:
                 picked_times_mirror = scratch.tile([P, 2 * N], F32, name="picked_times_mirror")
@@ -70,29 +66,26 @@ def tile_scaleinvariantreconstructionloss_kernel(tc, x, query, offs, out):
                     sim[:, mirror : mirror + 1], picked_times_mirror[:], ones[:], start=True, stop=True
                 )
 
-            for piece, (image, first, columns) in enumerate(QUERY_PIECES):
-                if image == b:
-                    q_times_x = scratch.tile([P, S], F32, name="q_times_x")
-                    nc.vector.scalar_tensor_tensor(
-                        q_times_x[:, 0:columns],
-                        q_tiles[b][:, first : first + columns],
-                        1.0,
-                        x_tiles[b][:, first : first + columns],
-                        MULT,
-                        MULT,
-                        accum_out=dot_sums[:, piece : piece + 1],
-                    )
+            q_times_x = scratch.tile([P, S], F32, name="q_times_x")
+            nc.vector.scalar_tensor_tensor(
+                q_times_x[:],
+                q_tiles[b][:],
+                1.0,
+                x_tiles[b][:],
+                MULT,
+                MULT,
+                accum_out=dot_sums[:, b : b + 1],
+            )
 
         positive_sim = held.tile([P, PAIRS], F32, name="positive_sim")
         penalty_sums = held.tile([P, 1], F32, name="penalty_sums")
         nc.scalar.activation(positive_sim[:], sim[:], RELU, accum_out=penalty_sums[:])
 
-        pieces = len(QUERY_PIECES)
-        terms = psum.tile([1, pieces + 1], F32, name="terms")
-        nc.tensor.matmul(terms[:, pieces : pieces + 1], penalty_weight[:], penalty_sums[:], start=True, stop=True)
-        nc.tensor.matmul(terms[:, 0:pieces], dot_weight[:], dot_sums[:], start=True, stop=True)
+        terms = psum.tile([1, IMAGES + 1], F32, name="terms")
+        nc.tensor.matmul(terms[:, IMAGES : IMAGES + 1], penalty_weight[:], penalty_sums[:], start=True, stop=True)
+        nc.tensor.matmul(terms[:, 0:IMAGES], dot_weight[:], dot_sums[:], start=True, stop=True)
 
-        terms_copy = held.tile([1, pieces + 1], F32, name="terms_copy")
+        terms_copy = held.tile([1, IMAGES + 1], F32, name="terms_copy")
         loss = held.tile([1, 1], F32, name="loss")
         nc.vector.tensor_scalar(terms_copy[:], terms[:], 1.0, 1.0, MULT, ADD, accum_out=loss[:])
         nc.sync.dma_start(out, loss[:])

@@ -26,15 +26,20 @@ def tile_scaleinvariantreconstructionloss_kernel(tc, x, query, offs, out):
         tc.tile_pool(name="scratch", bufs=2) as scratch,
         tc.psum_pool(name="psum", bufs=1) as psum,
     ):
-        last_image = IMAGE_ORDER[-1]
         offsets = held.tile([P, N // 16], U16, name="offsets")
         nc.sync.dma_start(offsets[:], offs)
         x_tiles = [held.tile([P, S], F32, name=f"x{b}") for b in range(IMAGES)]
-        q_tiles = [held.tile([P, S], F32, name=f"q{b}") for b in range(IMAGES)]
-        for b in IMAGE_ORDER:
-            nc.sync.dma_start(x_tiles[b][:], x[b * P : (b + 1) * P, :])
-            query_queue = nc.sync if b == last_image else nc.scalar
-            query_queue.dma_start(q_tiles[b][:], query[b * P : (b + 1) * P, :])
+        q_pairs = [held.tile([P, 2, S], F32, name=f"q_pair{k}") for k in range(PAIRS)]
+        query_by_image = query.rearrange("(b w) s -> w b s", w=P)
+        for k in range(PAIRS):
+            mirror = IMAGES - 1 - k
+            nc.sync.dma_start(x_tiles[k][:], x[k * P : (k + 1) * P, :])
+            nc.sync.dma_start(x_tiles[mirror][:], x[mirror * P : (mirror + 1) * P, :])
+            if k < PAIRS - 1:
+                nc.scalar.dma_start(q_pairs[k][:], query_by_image[:, k : mirror + 1 : mirror - k, :])
+            else:
+                nc.scalar.dma_start(q_pairs[k][:, 0, :], query_by_image[:, k, :])
+                nc.sync.dma_start(q_pairs[k][:, 1, :], query_by_image[:, mirror, :])
 
         ones = held.tile([P, 1], F32, name="ones")
         nc.vector.memset(ones[:], 1.0)
@@ -69,7 +74,7 @@ def tile_scaleinvariantreconstructionloss_kernel(tc, x, query, offs, out):
             q_times_x = scratch.tile([P, S], F32, name="q_times_x")
             nc.vector.scalar_tensor_tensor(
                 q_times_x[:],
-                q_tiles[b][:],
+                q_pairs[min(b, mirror)][:, 0 if b < mirror else 1, :],
                 1.0,
                 x_tiles[b][:],
                 MULT,

@@ -27,7 +27,6 @@ def tile_scaleinvariantreconstructionloss_kernel(tc, x, query, offs, out):
         tc.psum_pool(name="psum", bufs=1) as psum,
     ):
         offsets = held.tile([P, N // 16], U16, name="offsets")
-        nc.sync.dma_start(offsets[:], offs)
         x_tiles = [held.tile([P, S], F32, name=f"x{b}") for b in range(IMAGES)]
         q_pairs = [held.tile([P, 2, S], F32, name=f"q_pair{k}") for k in range(PAIRS)]
         query_by_image = query.rearrange("(b w) s -> w b s", w=P)
@@ -35,6 +34,8 @@ def tile_scaleinvariantreconstructionloss_kernel(tc, x, query, offs, out):
             mirror = IMAGES - 1 - k
             nc.sync.dma_start(x_tiles[k][:], x[k * P : (k + 1) * P, :])
             nc.sync.dma_start(x_tiles[mirror][:], x[mirror * P : (mirror + 1) * P, :])
+            if k == 0:
+                nc.sync.dma_start(offsets[:], offs)
             if k < PAIRS - 1:
                 nc.scalar.dma_start(q_pairs[k][:], query_by_image[:, k : mirror + 1 : mirror - k, :])
             else:

@@ -49,8 +49,8 @@ def tile_scaleinvariantreconstructionloss_kernel(tc, x, query, offs, out):
         penalty_weight = held.tile([P, 1], F32, name="penalty_weight")
         nc.vector.memset(penalty_weight[:], 1.0 / SIMS)
 
-        dot_sums = held.tile([P, IMAGES], F32, name="dot_sums")
         sim = psum.tile([P, PAIRS], F32, name="sim")
+        dot_sums = []
 
         for b in IMAGE_ORDER:
             mirror = IMAGES - 1 - b
@@ -72,6 +72,8 @@ def tile_scaleinvariantreconstructionloss_kernel(tc, x, query, offs, out):
                     sim[:, mirror : mirror + 1], picked_times_mirror[:], ones[:], start=True, stop=True
                 )
 
+            dot_sum = held.tile([P, 1], F32, name=f"dot_sum{b}")
+            dot_sums.append(dot_sum)
             q_times_x = scratch.tile([P, S], F32, name="q_times_x")
             nc.vector.scalar_tensor_tensor(
                 q_times_x[:],
@@ -80,18 +82,19 @@ def tile_scaleinvariantreconstructionloss_kernel(tc, x, query, offs, out):
                 x_tiles[b][:],
                 MULT,
                 MULT,
-                accum_out=dot_sums[:, b : b + 1],
+                accum_out=dot_sum[:],
             )
 
         positive_sim = held.tile([P, PAIRS], F32, name="positive_sim")
         penalty_sums = held.tile([P, 1], F32, name="penalty_sums")
         nc.scalar.activation(positive_sim[:], sim[:], RELU, accum_out=penalty_sums[:])
 
-        terms = psum.tile([1, IMAGES + 1], F32, name="terms")
-        nc.tensor.matmul(terms[:, IMAGES : IMAGES + 1], penalty_weight[:], penalty_sums[:], start=True, stop=True)
-        nc.tensor.matmul(terms[:, 0:IMAGES], dot_weight[:], dot_sums[:], start=True, stop=True)
+        total = psum.tile([1, 1], F32, name="total")
+        for i, dot_sum in enumerate(dot_sums[:-1]):
+            nc.tensor.matmul(total[:], dot_weight[:], dot_sum[:], start=i == 0, stop=False)
+        nc.tensor.matmul(total[:], penalty_weight[:], penalty_sums[:], start=False, stop=False)
+        nc.tensor.matmul(total[:], dot_weight[:], dot_sums[-1][:], start=False, stop=True)
 
-        terms_copy = held.tile([1, IMAGES + 1], F32, name="terms_copy")
         loss = held.tile([1, 1], F32, name="loss")
-        nc.vector.tensor_scalar(terms_copy[:], terms[:], 1.0, 1.0, MULT, ADD, accum_out=loss[:])
+        nc.vector.tensor_scalar_add(loss[:], total[:], 1.0)
         nc.sync.dma_start(out, loss[:])

import concourse.mybir as mybir

F32 = mybir.dt.float32
U16 = mybir.dt.uint16
MULT = mybir.AluOpType.mult
ADD = mybir.AluOpType.add
RELU = mybir.ActivationFunctionType.Relu

P = 128
IMAGES = 8
PAIRS = IMAGES // 2
S = 1024
N = 64
PLACES = 65536
SIMS = IMAGES * N

IMAGE_ORDER = [b for k in range(PAIRS) for b in (k, IMAGES - 1 - k)]

FLOPS = 2 * IMAGES * P * S + 2 * IMAGES * P * N


def tile_scaleinvariantreconstructionloss_kernel(tc, x, query, offs, out):
    nc = tc.nc
    with (
        tc.tile_pool(name="held", bufs=1) as held,
        tc.tile_pool(name="scratch", bufs=2) as scratch,
        tc.psum_pool(name="psum", bufs=1) as psum,
    ):
        offsets = held.tile([P, N // 16], U16, name="offsets")
        x_tiles = [held.tile([P, S], F32, name=f"x{b}") for b in range(IMAGES)]
        q_pairs = [held.tile([P, 2, S], F32, name=f"q_pair{k}") for k in range(PAIRS)]
        query_by_image = query.rearrange("(b w) s -> w b s", w=P)
        for k in range(PAIRS):
            mirror = IMAGES - 1 - k
            nc.sync.dma_start(x_tiles[k][:], x[k * P : (k + 1) * P, :])
            nc.sync.dma_start(x_tiles[mirror][:], x[mirror * P : (mirror + 1) * P, :])
            if k == 0:
                nc.sync.dma_start(offsets[:], offs)
            if k < PAIRS - 1:
                nc.scalar.dma_start(q_pairs[k][:], query_by_image[:, k : mirror + 1 : mirror - k, :])
            else:
                nc.scalar.dma_start(q_pairs[k][:, 0, :], query_by_image[:, k, :])
                nc.sync.dma_start(q_pairs[k][:, 1, :], query_by_image[:, mirror, :])

        ones = held.tile([P, 1], F32, name="ones")
        nc.vector.memset(ones[:], 1.0)
        dot_weight = held.tile([P, 1], F32, name="dot_weight")
        nc.vector.memset(dot_weight[:], -1.0 / PLACES)
        penalty_weight = held.tile([P, 1], F32, name="penalty_weight")
        nc.vector.memset(penalty_weight[:], 1.0 / SIMS)

        sim = psum.tile([P, PAIRS], F32, name="sim")
        dot_sums = []

        for b in IMAGE_ORDER:
            mirror = IMAGES - 1 - b
            if mirror < b:
                picked_times_mirror = scratch.tile([P, 2 * N], F32, name="picked_times_mirror")
                nc.vector.tensor_tensor(
                    picked_times_mirror[:, 0:N],
                    x_tiles[mirror][:].indirect(offsets[:]),
                    x_tiles[b][:, 0:N],
                    MULT,
                )
                nc.vector.tensor_tensor(
                    picked_times_mirror[:, N : 2 * N],
                    x_tiles[b][:].indirect(offsets[:]),
                    x_tiles[mirror][:, 0:N],
                    MULT,
                )
                nc.tensor.matmul(
                    sim[:, mirror : mirror + 1], picked_times_mirror[:], ones[:], start=True, stop=True
                )

            dot_sum = held.tile([P, 1], F32, name=f"dot_sum{b}")
            dot_sums.append(dot_sum)
            q_times_x = scratch.tile([P, S], F32, name="q_times_x")
            nc.vector.scalar_tensor_tensor(
                q_times_x[:],
                q_pairs[min(b, mirror)][:, 0 if b < mirror else 1, :],
                1.0,
                x_tiles[b][:],
                MULT,
                MULT,
                accum_out=dot_sum[:],
            )

        positive_sim = held.tile([P, PAIRS], F32, name="positive_sim")
        penalty_sums = held.tile([P, 1], F32, name="penalty_sums")
        nc.scalar.activation(positive_sim[:], sim[:], RELU, accum_out=penalty_sums[:])

        total = psum.tile([1, 1], F32, name="total")
        for i, dot_sum in enumerate(dot_sums[:-1]):
            nc.tensor.matmul(total[:], dot_weight[:], dot_sum[:], start=i == 0, stop=False)
        nc.tensor.matmul(total[:], penalty_weight[:], penalty_sums[:], start=False, stop=False)
        nc.tensor.matmul(total[:], dot_weight[:], dot_sums[-1][:], start=False, stop=True)

        loss = held.tile([1, 1], F32, name="loss")
        nc.vector.tensor_scalar_add(loss[:], total[:], 1.0)
        nc.sync.dma_start(out, loss[:])
